import numpy as np
import ml_dtypes


def mxq(x, axis, fmt="e4m3"):
    dtype, down = {"e4m3": (ml_dtypes.float8_e4m3fn, 7), "e5m2": (ml_dtypes.float8_e5m2, 14)}[fmt]
    v = np.moveaxis(np.asarray(x, np.float32).astype(ml_dtypes.bfloat16).astype(np.float64), axis, -1)
    blocks = v.reshape(v.shape[:-1] + (-1, 32))
    amax = np.abs(blocks).max(-1, keepdims=True)
    byte = np.maximum(np.where(amax > 0, np.frexp(amax)[1] - 1 + 127, 0) - down, 1)
    scale = np.exp2(byte - 127.0)
    codes = (blocks / scale).astype(np.float32).astype(dtype).astype(np.float64)
    return np.moveaxis((codes * scale).reshape(v.shape), -1, axis)


WIDE = False


def mx_kscale(k):
    if not WIDE:
        return np.ones(k)
    levels = np.array([10, -10, 5, -5, 0])
    a = np.random.permutation(np.resize(levels, k // 512 * 4)).reshape(k // 512, 4)
    idx = np.arange(k)
    return np.exp2(a[idx // 512, idx % 128 // 32])


BF16 = ml_dtypes.bfloat16


def bf(x):
    return np.asarray(x, np.float32).astype(BF16)


def f64(x):
    return np.asarray(x).astype(np.float64)


B, T, D, H = 1, 128, 1024, 16
HD = D // H
SCALE = HD ** (-0.5)


def rotate_half(u):
    u1, u2 = np.split(u, 2, axis=-1)
    return np.concatenate([-u2, u1], axis=-1)


def apply_rope(u, sin, cos):
    return u * cos[None, :, None, :] + rotate_half(u) * sin[None, :, None, :]


def setup_inputs():
    s = mx_kscale(D)
    return {"x": bf(np.random.standard_normal((B, T, D)) * s),
            "sin": bf(np.random.standard_normal((T, HD))),
            "cos": bf(np.random.standard_normal((T, HD))),
            "W_qkv": bf(np.random.standard_normal((D, D + 2 * HD)) * 2.0 / np.sqrt(D) / s[:, None])}


def reference(x, sin, cos, W_qkv):
    sin, cos = f64(sin), f64(cos)
    qkv = mxq(f64(x), 2, "e4m3") @ mxq(f64(W_qkv), 0, "e4m3")
    q, k, v = np.split(qkv, [D, D + HD], axis=-1)
    q = q.reshape(B, T, H, HD) * SCALE
    q_rot = np.ascontiguousarray(apply_rope(q, sin, cos).transpose(0, 2, 1, 3))
    k_rot = apply_rope(k[:, :, None, :], sin, cos)[:, :, 0, :]
    return q_rot, k_rot, v

@@ -1,0 +1,171 @@
+from contextlib import ExitStack
+
+import concourse.mybir as mybir
+from concourse.masks import make_identity
+
+BF16 = mybir.dt.bfloat16
+F32 = mybir.dt.float32
+U32 = mybir.dt.uint32
+U8 = mybir.dt.uint8
+FP8X4 = mybir.dt.float8_e4m3fn_x4
+MULT = mybir.AluOpType.mult
+ADD = mybir.AluOpType.add
+
+P = 128
+PACK = 4
+K_PASS = P * PACK
+K = 1024
+PASSES = K // K_PASS
+HEADS = 16
+HEAD_DIM = 64
+HALF = HEAD_DIM // 2
+Q_COLS = HEADS * HEAD_DIM
+N_COLS = Q_COLS + 2 * HEAD_DIM
+Q_SCALE = HEAD_DIM**-0.5
+
+LOAD_COLS = 512
+STEP_COLS = 256
+RUN = 4
+VECTOR_SHARE = 4
+
+FLOPS = 2 * P * K * N_COLS
+
+
+def regroup(nc, grouped, raw):
+    width = raw.shape[2]
+    border = width - width // VECTOR_SHARE
+    nc.scalar.copy(
+        out=grouped[:, :border, :].rearrange("p (c i) j -> p c j i", i=RUN),
+        in_=raw[:, :, :border].rearrange("p j (c i) -> p c j i", i=RUN),
+    )
+    nc.vector.tensor_copy(
+        out=grouped[:, border:, :].rearrange("p (c i) j -> p c j i", i=RUN),
+        in_=raw[:, :, border:].rearrange("p j (c i) -> p c j i", i=RUN),
+    )
+
+
+def rope(nc, pool, label, acc, cos_sb, sin_sb, scale):
+    heads = acc.shape[1]
+    low = slice(0, HALF)
+    high = slice(HALF, HEAD_DIM)
+
+    def for_all_heads(table):
+        return table.unsqueeze(1).to_broadcast([P, heads, table.shape[1]])
+
+    straight = pool.tile([P, heads, HEAD_DIM], F32, name="straight_" + label)
+    crossed = pool.tile([P, heads, HEAD_DIM], F32, name="crossed_" + label)
+    rotated = pool.tile([P, heads, HEAD_DIM], F32, name="rotated_" + label)
+    nc.vector.scalar_tensor_tensor(
+        out=crossed[:, :, low],
+        in0=acc[:, :, high],
+        scalar=-scale,
+        in1=for_all_heads(sin_sb[:, low]),
+        op0=MULT,
+        op1=MULT,
+    )
+    nc.vector.scalar_tensor_tensor(
+        out=crossed[:, :, high],
+        in0=acc[:, :, low],
+        scalar=scale,
+        in1=for_all_heads(sin_sb[:, high]),
+        op0=MULT,
+        op1=MULT,
+    )
+    nc.vector.scalar_tensor_tensor(
+        out=straight[:],
+        in0=acc,
+        scalar=scale,
+        in1=for_all_heads(cos_sb[:]),
+        op0=MULT,
+        op1=MULT,
+    )
+    nc.vector.tensor_tensor(out=rotated[:], in0=straight[:], in1=crossed[:], op=ADD)
+    return rotated
+
+
+def tile_multiqueryattention_pa_s_kernel(tc, x, sin, cos, w_qkv, q_rot, k_rot, v_out):
+    nc = tc.nc
+    with ExitStack() as ctx:
+        keep = ctx.enter_context(tc.tile_pool(name="keep", bufs=1))
+        psum = ctx.enter_context(tc.psum_pool(name="psum", bufs=1))
+
+        x_sb = keep.tile([P, K], BF16)
+        nc.sync.dma_start(out=x_sb[:], in_=x[0])
+        cos_sb = keep.tile([P, HEAD_DIM], BF16)
+        nc.scalar.dma_start(out=cos_sb[:], in_=cos)
+        sin_sb = keep.tile([P, HEAD_DIM], BF16)
+        nc.scalar.dma_start(out=sin_sb[:], in_=sin)
+
+        raw_of_load = []
+        for first in range(0, N_COLS, LOAD_COLS):
+            width = min(LOAD_COLS, N_COLS - first)
+            raw = keep.tile([P, PASSES, PACK, width], BF16, name="raw%d" % first)
+            for g in range(PASSES):
+                nc.sync.dma_start(
+                    out=raw[:, g, :, :],
+                    in_=w_qkv[g * K_PASS : (g + 1) * K_PASS, first : first + width].rearrange(
+                        "(p j) w -> p j w", j=PACK
+                    ),
+                )
+            raw_of_load.append(raw)
+
+        identity = keep.tile([P, P], F32)
+        make_identity(nc, identity[:])
+        x_words = x_sb[:].bitcast(F32).rearrange("t (g p u) -> t g u p", g=PASSES, u=PACK // 2)
+        x_turned = psum.tile([P, PASSES, PACK // 2, P], F32)
+        for g in range(PASSES):
+            for u in range(PACK // 2):
+                nc.tensor.transpose(x_turned[:, g, u, :], x_words[:, g, u, :], identity[:])
+        x_grouped = keep.tile([P, PASSES, P, PACK // 2], F32, align_bytes=64)
+        nc.scalar.copy(out=x_grouped[:], in_=x_turned[:].rearrange("p g u t -> p g t u"))
+        x_codes = keep.tile([P, PASSES, P], U32, align_bytes=64)
+        x_scales = keep.tile([P, PASSES, P], U8, align_bytes=64)
+        nc.vector.quantize_mx(
+            out=x_codes[:].rearrange("p g t -> p (g t)").bitcast(FP8X4),
+            scales=x_scales[:].rearrange("p g t -> p (g t)"),
+            in_=x_grouped[:].rearrange("p g t u -> p (g t u)").bitcast(BF16),
+        )
+
+        for first in range(0, N_COLS, STEP_COLS):
+            width = min(STEP_COLS, N_COLS - first)
+            raw = raw_of_load[first // LOAD_COLS]
+            in_load = slice(first % LOAD_COLS, first % LOAD_COLS + width)
+
+            grouped = keep.tile([P, PASSES, width, PACK], BF16, align_bytes=64, name="grouped%d" % first)
+            w_codes = keep.tile([P, PASSES, width], U32, align_bytes=64, name="w_codes%d" % first)
+            w_scales = keep.tile([P, PASSES, width], U8, align_bytes=64, name="w_scales%d" % first)
+            for g in range(PASSES):
+                regroup(nc, grouped[:, g, :, :], raw[:, g, :, in_load])
+            for g in range(PASSES):
+                nc.vector.quantize_mx(
+                    out=w_codes[:, g, :].bitcast(FP8X4),
+                    scales=w_scales[:, g, :],
+                    in_=grouped[:, g, :, :].rearrange("p w j -> p (w j)"),
+                )
+
+            acc = psum.tile([P, width], F32, name="acc%d" % first)
+            for g in range(PASSES):
+                nc.tensor.matmul_mx(
+                    out=acc[:],
+                    lhsT=x_codes[:, g, :].bitcast(FP8X4),
+                    lhsT_scale=x_scales[:, g, :],
+                    rhs=w_codes[:, g, :].bitcast(FP8X4),
+                    rhs_scale=w_scales[:, g, :],
+                    start=(g == 0),
+                    stop=(g == PASSES - 1),
+                )
+            acc_heads = acc[:].rearrange("t (h d) -> t h d", d=HEAD_DIM)
+
+            if first < Q_COLS:
+                head = first // HEAD_DIM
+                rotated = rope(nc, keep, "q%d" % first, acc_heads, cos_sb, sin_sb, Q_SCALE)
+                nc.sync.dma_start(
+                    out=q_rot[0, head : head + width // HEAD_DIM].rearrange("h t d -> t h d"),
+                    in_=rotated[:],
+                )
+            else:
+                rotated = rope(nc, keep, "k", acc_heads[:, 0:1, :], cos_sb, sin_sb, 1.0)
+                nc.sync.dma_start(out=k_rot[0], in_=rotated[:, 0, :])
+                v_sb = keep.tile([P, HEAD_DIM], F32)
+                nc.vector.tensor_copy(out=v_sb[:], in_=acc_heads[:, 1, :])
+                nc.sync.dma_start(out=v_out[0], in_=v_sb[:])

@@ -23,17 +23,16 @@ Q_COLS = HEADS * HEAD_DIM
 N_COLS = Q_COLS + 2 * HEAD_DIM
 Q_SCALE = HEAD_DIM**-0.5
 
-LOAD_COLS = 512
 STEP_COLS = 256
 RUN = 4
-VECTOR_SHARE = 4
+VECTOR_PARTS = 4
 
 FLOPS = 2 * P * K * N_COLS
 
 
 def regroup(nc, grouped, raw):
     width = raw.shape[2]
-    border = width - width // VECTOR_SHARE
+    border = width - width * VECTOR_PARTS // 16
     nc.scalar.copy(
         out=grouped[:, :border, :].rearrange("p (c i) j -> p c j i", i=RUN),
         in_=raw[:, :, :border].rearrange("p j (c i) -> p c j i", i=RUN),
@@ -44,50 +43,20 @@ def regroup(nc, grouped, raw):
     )
 
 
-def rope(nc, pool, label, acc, cos_sb, sin_sb, scale):
-    heads = acc.shape[1]
+def tile_multiqueryattention_pa_s_kernel(tc, x, sin, cos, w_qkv, q_rot, k_rot, v_out):
+    nc = tc.nc
+    steps = []
+    for first in range(0, Q_COLS, STEP_COLS):
+        steps.append((first, STEP_COLS, STEP_COLS // HEAD_DIM, Q_SCALE))
+    steps.append((Q_COLS, 2 * HEAD_DIM, 1, 1.0))
+    n_steps = len(steps)
     low = slice(0, HALF)
     high = slice(HALF, HEAD_DIM)
 
-    def for_all_heads(table):
-        return table.unsqueeze(1).to_broadcast([P, heads, table.shape[1]])
-
-    straight = pool.tile([P, heads, HEAD_DIM], F32, name="straight_" + label)
-    crossed = pool.tile([P, heads, HEAD_DIM], F32, name="crossed_" + label)
-    rotated = pool.tile([P, heads, HEAD_DIM], F32, name="rotated_" + label)
-    nc.vector.scalar_tensor_tensor(
-        out=crossed[:, :, low],
-        in0=acc[:, :, high],
-        scalar=-scale,
-        in1=for_all_heads(sin_sb[:, low]),
-        op0=MULT,
-        op1=MULT,
-    )
-    nc.vector.scalar_tensor_tensor(
-        out=crossed[:, :, high],
-        in0=acc[:, :, low],
-        scalar=scale,
-        in1=for_all_heads(sin_sb[:, high]),
-        op0=MULT,
-        op1=MULT,
-    )
-    nc.vector.scalar_tensor_tensor(
-        out=straight[:],
-        in0=acc,
-        scalar=scale,
-        in1=for_all_heads(cos_sb[:]),
-        op0=MULT,
-        op1=MULT,
-    )
-    nc.vector.tensor_tensor(out=rotated[:], in0=straight[:], in1=crossed[:], op=ADD)
-    return rotated
-
-
-def tile_multiqueryattention_pa_s_kernel(tc, x, sin, cos, w_qkv, q_rot, k_rot, v_out):
-    nc = tc.nc
     with ExitStack() as ctx:
         keep = ctx.enter_context(tc.tile_pool(name="keep", bufs=1))
         psum = ctx.enter_context(tc.psum_pool(name="psum", bufs=1))
+        ctx.enter_context(tc.manual_schedule())
 
         x_sb = keep.tile([P, K], BF16)
         nc.sync.dma_start(out=x_sb[:], in_=x[0])
@@ -96,18 +65,17 @@ def tile_multiqueryattention_pa_s_kernel(tc, x, sin, cos, w_qkv, q_rot, k_rot, v
         sin_sb = keep.tile([P, HEAD_DIM], BF16)
         nc.scalar.dma_start(out=sin_sb[:], in_=sin)
 
-        raw_of_load = []
-        for first in range(0, N_COLS, LOAD_COLS):
-            width = min(LOAD_COLS, N_COLS - first)
-            raw = keep.tile([P, PASSES, PACK, width], BF16, name="raw%d" % first)
+        raw = []
+        for first, width, heads, scale in steps:
+            raw_step = keep.tile([P, PASSES, PACK, width], BF16, name="raw%d" % first)
             for g in range(PASSES):
                 nc.sync.dma_start(
-                    out=raw[:, g, :, :],
+                    out=raw_step[:, g, :, :],
                     in_=w_qkv[g * K_PASS : (g + 1) * K_PASS, first : first + width].rearrange(
                         "(p j) w -> p j w", j=PACK
                     ),
                 )
-            raw_of_load.append(raw)
+            raw.append(raw_step)
 
         identity = keep.tile([P, P], F32)
         make_identity(nc, identity[:])
@@ -117,55 +85,97 @@ def tile_multiqueryattention_pa_s_kernel(tc, x, sin, cos, w_qkv, q_rot, k_rot, v
             for u in range(PACK // 2):
                 nc.tensor.transpose(x_turned[:, g, u, :], x_words[:, g, u, :], identity[:])
         x_grouped = keep.tile([P, PASSES, P, PACK // 2], F32, align_bytes=64)
-        nc.scalar.copy(out=x_grouped[:], in_=x_turned[:].rearrange("p g u t -> p g t u"))
+        nc.vector.tensor_copy(out=x_grouped[:], in_=x_turned[:].rearrange("p g u t -> p g t u"))
         x_codes = keep.tile([P, PASSES, P], U32, align_bytes=64)
         x_scales = keep.tile([P, PASSES, P], U8, align_bytes=64)
-        nc.vector.quantize_mx(
-            out=x_codes[:].rearrange("p g t -> p (g t)").bitcast(FP8X4),
-            scales=x_scales[:].rearrange("p g t -> p (g t)"),
-            in_=x_grouped[:].rearrange("p g t u -> p (g t u)").bitcast(BF16),
-        )
 
-        for first in range(0, N_COLS, STEP_COLS):
-            width = min(STEP_COLS, N_COLS - first)
-            raw = raw_of_load[first // LOAD_COLS]
-            in_load = slice(first % LOAD_COLS, first % LOAD_COLS + width)
+        def quantise_x():
+            nc.vector.quantize_mx(
+                out=x_codes[:].rearrange("p g t -> p (g t)").bitcast(FP8X4),
+                scales=x_scales[:].rearrange("p g t -> p (g t)"),
+                in_=x_grouped[:].rearrange("p g t u -> p (g t u)").bitcast(BF16),
+            )
 
-            grouped = keep.tile([P, PASSES, width, PACK], BF16, align_bytes=64, name="grouped%d" % first)
-            w_codes = keep.tile([P, PASSES, width], U32, align_bytes=64, name="w_codes%d" % first)
-            w_scales = keep.tile([P, PASSES, width], U8, align_bytes=64, name="w_scales%d" % first)
+        grouped = []
+        w_codes = []
+        w_scales = []
+        acc = []
+        straight = []
+        crossed = []
+        rotated = []
+        for first, width, heads, scale in steps:
+            grouped.append(keep.tile([P, PASSES, width, PACK], BF16, align_bytes=64, name="grouped%d" % first))
+            w_codes.append(keep.tile([P, PASSES, width], U32, align_bytes=64, name="w_codes%d" % first))
+            w_scales.append(keep.tile([P, PASSES, width], U8, align_bytes=64, name="w_scales%d" % first))
+            acc.append(psum.tile([P, width // HEAD_DIM, HEAD_DIM], F32, name="acc%d" % first))
+            straight.append(keep.tile([P, heads, HEAD_DIM], F32, name="straight%d" % first))
+            crossed.append(keep.tile([P, heads, HEAD_DIM], F32, name="crossed%d" % first))
+            rotated.append(keep.tile([P, heads, HEAD_DIM], F32, name="rotated%d" % first))
+        v_sb = keep.tile([P, HEAD_DIM], F32)
+
+        def regroup_step(s):
             for g in range(PASSES):
-                regroup(nc, grouped[:, g, :, :], raw[:, g, :, in_load])
-            for g in range(PASSES):
-                nc.vector.quantize_mx(
-                    out=w_codes[:, g, :].bitcast(FP8X4),
-                    scales=w_scales[:, g, :],
-                    in_=grouped[:, g, :, :].rearrange("p w j -> p (w j)"),
-                )
+                regroup(nc, grouped[s][:, g, :, :], raw[s][:, g, :, :])
 
-            acc = psum.tile([P, width], F32, name="acc%d" % first)
+        def quantise_and_multiply(s):
+            nc.vector.quantize_mx(
+                out=w_codes[s][:].rearrange("p g w -> p (g w)").bitcast(FP8X4),
+                scales=w_scales[s][:].rearrange("p g w -> p (g w)"),
+                in_=grouped[s][:].rearrange("p g w j -> p (g w j)"),
+            )
             for g in range(PASSES):
                 nc.tensor.matmul_mx(
-                    out=acc[:],
+                    out=acc[s][:].rearrange("t h d -> t (h d)"),
                     lhsT=x_codes[:, g, :].bitcast(FP8X4),
                     lhsT_scale=x_scales[:, g, :],
-                    rhs=w_codes[:, g, :].bitcast(FP8X4),
-                    rhs_scale=w_scales[:, g, :],
+                    rhs=w_codes[s][:, g, :].bitcast(FP8X4),
+                    rhs_scale=w_scales[s][:, g, :],
                     start=(g == 0),
                     stop=(g == PASSES - 1),
                 )
-            acc_heads = acc[:].rearrange("t (h d) -> t h d", d=HEAD_DIM)
 
-            if first < Q_COLS:
-                head = first // HEAD_DIM
-                rotated = rope(nc, keep, "q%d" % first, acc_heads, cos_sb, sin_sb, Q_SCALE)
-                nc.sync.dma_start(
-                    out=q_rot[0, head : head + width // HEAD_DIM].rearrange("h t d -> t h d"),
-                    in_=rotated[:],
-                )
-            else:
-                rotated = rope(nc, keep, "k", acc_heads[:, 0:1, :], cos_sb, sin_sb, 1.0)
-                nc.sync.dma_start(out=k_rot[0], in_=rotated[:, 0, :])
-                v_sb = keep.tile([P, HEAD_DIM], F32)
-                nc.vector.tensor_copy(out=v_sb[:], in_=acc_heads[:, 1, :])
+        def rope_products(s):
+            first, width, heads, scale = steps[s]
+            u = acc[s][:, 0:heads, :]
+
+            def for_all_heads(table):
+                return table.unsqueeze(1).to_broadcast([P, heads, table.shape[1]])
+
+            nc.vector.scalar_tensor_tensor(
+                out=crossed[s][:, :, low], in0=u[:, :, high], scalar=-scale,
+                in1=for_all_heads(sin_sb[:, low]), op0=MULT, op1=MULT,
+            )
+            nc.vector.scalar_tensor_tensor(
+                out=crossed[s][:, :, high], in0=u[:, :, low], scalar=scale,
+                in1=for_all_heads(sin_sb[:, high]), op0=MULT, op1=MULT,
+            )
+            nc.vector.scalar_tensor_tensor(
+                out=straight[s][:], in0=u, scalar=scale,
+                in1=for_all_heads(cos_sb[:]), op0=MULT, op1=MULT,
+            )
+            if first == Q_COLS:
+                nc.vector.tensor_copy(out=v_sb[:], in_=acc[s][:, 1, :])
+
+        def rope_sum_and_store(s):
+            first, width, heads, scale = steps[s]
+            nc.vector.tensor_tensor(out=rotated[s][:], in0=straight[s][:], in1=crossed[s][:], op=ADD)
+            if first == Q_COLS:
+                nc.sync.dma_start(out=k_rot[0], in_=rotated[s][:, 0, :])
                 nc.sync.dma_start(out=v_out[0], in_=v_sb[:])
+            else:
+                head = first // HEAD_DIM
+                nc.sync.dma_start(
+                    out=q_rot[0, head : head + heads].rearrange("h t d -> t h d"), in_=rotated[s][:]
+                )
+
+        for s in range(n_steps + 2):
+            if 1 <= s <= n_steps:
+                quantise_and_multiply(s - 1)
+            if s >= 2:
+                rope_products(s - 2)
+            if s < n_steps:
+                regroup_step(s)
+            if s == 0:
+                quantise_x()
+            if s >= 2:
+                rope_sum_and_store(s - 2)

@@ -25,30 +25,25 @@ Q_SCALE = HEAD_DIM**-0.5
 
 STEP_COLS = 256
 RUN = 4
-VECTOR_PARTS = 4
+VECTOR_PARTS = ((8, 8), (8, 8), (0, 8), (0, 4), (0, 0))
 
 FLOPS = 2 * P * K * N_COLS
 
 
-def regroup(nc, grouped, raw):
-    width = raw.shape[2]
-    border = width - width * VECTOR_PARTS // 16
-    nc.scalar.copy(
-        out=grouped[:, :border, :].rearrange("p (c i) j -> p c j i", i=RUN),
-        in_=raw[:, :, :border].rearrange("p j (c i) -> p c j i", i=RUN),
-    )
-    nc.vector.tensor_copy(
-        out=grouped[:, border:, :].rearrange("p (c i) j -> p c j i", i=RUN),
-        in_=raw[:, :, border:].rearrange("p j (c i) -> p c j i", i=RUN),
-    )
+def interleaved(grouped):
+    return grouped.rearrange("p (c i) j -> p c j i", i=RUN)
+
+
+def rows(raw):
+    return raw.rearrange("p j (c i) -> p c j i", i=RUN)
 
 
 def tile_multiqueryattention_pa_s_kernel(tc, x, sin, cos, w_qkv, q_rot, k_rot, v_out):
     nc = tc.nc
     steps = []
     for first in range(0, Q_COLS, STEP_COLS):
-        steps.append((first, STEP_COLS, STEP_COLS // HEAD_DIM, Q_SCALE))
-    steps.append((Q_COLS, 2 * HEAD_DIM, 1, 1.0))
+        steps.append((first, STEP_COLS, STEP_COLS // HEAD_DIM))
+    steps.append((Q_COLS, 2 * HEAD_DIM, 1))
     n_steps = len(steps)
     low = slice(0, HALF)
     high = slice(HALF, HEAD_DIM)
@@ -58,24 +53,31 @@ def tile_multiqueryattention_pa_s_kernel(tc, x, sin, cos, w_qkv, q_rot, k_rot, v
         psum = ctx.enter_context(tc.psum_pool(name="psum", bufs=1))
         ctx.enter_context(tc.manual_schedule())
 
+        raw = []
+
+        def load_step(s):
+            first, width, heads = steps[s]
+            tiles = []
+            for g in range(PASSES):
+                raw_pass = keep.tile([P, PACK, width], BF16, name="raw%d_%d" % (first, g))
+                nc.sync.dma_start(
+                    out=raw_pass[:],
+                    in_=w_qkv[g * K_PASS : (g + 1) * K_PASS, first : first + width].rearrange(
+                        "(p j) w -> p j w", j=PACK
+                    ),
+                )
+                tiles.append(raw_pass)
+            raw.append(tiles)
+
+        load_step(0)
         x_sb = keep.tile([P, K], BF16)
         nc.sync.dma_start(out=x_sb[:], in_=x[0])
         cos_sb = keep.tile([P, HEAD_DIM], BF16)
         nc.scalar.dma_start(out=cos_sb[:], in_=cos)
         sin_sb = keep.tile([P, HEAD_DIM], BF16)
         nc.scalar.dma_start(out=sin_sb[:], in_=sin)
-
-        raw = []
-        for first, width, heads, scale in steps:
-            raw_step = keep.tile([P, PASSES, PACK, width], BF16, name="raw%d" % first)
-            for g in range(PASSES):
-                nc.sync.dma_start(
-                    out=raw_step[:, g, :, :],
-                    in_=w_qkv[g * K_PASS : (g + 1) * K_PASS, first : first + width].rearrange(
-                        "(p j) w -> p j w", j=PACK
-                    ),
-                )
-            raw.append(raw_step)
+        for s in range(1, n_steps):
+            load_step(s)
 
         identity = keep.tile([P, P], F32)
         make_identity(nc, identity[:])
@@ -85,9 +87,11 @@ def tile_multiqueryattention_pa_s_kernel(tc, x, sin, cos, w_qkv, q_rot, k_rot, v
             for u in range(PACK // 2):
                 nc.tensor.transpose(x_turned[:, g, u, :], x_words[:, g, u, :], identity[:])
         x_grouped = keep.tile([P, PASSES, P, PACK // 2], F32, align_bytes=64)
-        nc.vector.tensor_copy(out=x_grouped[:], in_=x_turned[:].rearrange("p g u t -> p g t u"))
         x_codes = keep.tile([P, PASSES, P], U32, align_bytes=64)
         x_scales = keep.tile([P, PASSES, P], U8, align_bytes=64)
+
+        def regroup_x():
+            nc.vector.tensor_copy(out=x_grouped[:], in_=x_turned[:].rearrange("p g u t -> p g t u"))
 
         def quantise_x():
             nc.vector.quantize_mx(
@@ -96,26 +100,44 @@ def tile_multiqueryattention_pa_s_kernel(tc, x, sin, cos, w_qkv, q_rot, k_rot, v
                 in_=x_grouped[:].rearrange("p g t u -> p (g t u)").bitcast(BF16),
             )
 
+        k_factors = keep.tile([P, 2, HEAD_DIM], F32)
+        nc.gpsimd.tensor_copy(out=k_factors[:, 0, :], in_=cos_sb[:])
+        nc.gpsimd.tensor_copy(out=k_factors[:, 1, low], in_=sin_sb[:, high])
+        nc.gpsimd.tensor_scalar(
+            out=k_factors[:, 1, high], in0=sin_sb[:, low], scalar1=-1.0, scalar2=0.0, op0=MULT, op1=ADD
+        )
+        q_factors = keep.tile([P, 2, HEAD_DIM], F32)
+        nc.gpsimd.tensor_scalar(
+            out=q_factors[:], in0=k_factors[:], scalar1=Q_SCALE, scalar2=0.0, op0=MULT, op1=ADD
+        )
+
         grouped = []
         w_codes = []
         w_scales = []
         acc = []
-        straight = []
-        crossed = []
+        products = []
         rotated = []
-        for first, width, heads, scale in steps:
+        for first, width, heads in steps:
             grouped.append(keep.tile([P, PASSES, width, PACK], BF16, align_bytes=64, name="grouped%d" % first))
             w_codes.append(keep.tile([P, PASSES, width], U32, align_bytes=64, name="w_codes%d" % first))
             w_scales.append(keep.tile([P, PASSES, width], U8, align_bytes=64, name="w_scales%d" % first))
             acc.append(psum.tile([P, width // HEAD_DIM, HEAD_DIM], F32, name="acc%d" % first))
-            straight.append(keep.tile([P, heads, HEAD_DIM], F32, name="straight%d" % first))
-            crossed.append(keep.tile([P, heads, HEAD_DIM], F32, name="crossed%d" % first))
+            products.append(keep.tile([P, heads, 2, HEAD_DIM], F32, name="products%d" % first))
             rotated.append(keep.tile([P, heads, HEAD_DIM], F32, name="rotated%d" % first))
         v_sb = keep.tile([P, HEAD_DIM], F32)
 
-        def regroup_step(s):
-            for g in range(PASSES):
-                regroup(nc, grouped[s][:, g, :, :], raw[s][:, g, :, :])
+        def border(s, g):
+            width = steps[s][1]
+            return width - width * VECTOR_PARTS[s][g] // 16
+
+        def regroup_scalar(s, g):
+            b = border(s, g)
+            nc.scalar.copy(out=interleaved(grouped[s][:, g, :b, :]), in_=rows(raw[s][g][:, :, :b]))
+
+        def regroup_vector(s, g):
+            b = border(s, g)
+            if b < steps[s][1]:
+                nc.vector.tensor_copy(out=interleaved(grouped[s][:, g, b:, :]), in_=rows(raw[s][g][:, :, b:]))
 
         def quantise_and_multiply(s):
             nc.vector.quantize_mx(
@@ -123,6 +145,8 @@ def tile_multiqueryattention_pa_s_kernel(tc, x, sin, cos, w_qkv, q_rot, k_rot, v
                 scales=w_scales[s][:].rearrange("p g w -> p (g w)"),
                 in_=grouped[s][:].rearrange("p g w j -> p (g w j)"),
             )
+
+        def multiply(s):
             for g in range(PASSES):
                 nc.tensor.matmul_mx(
                     out=acc[s][:].rearrange("t h d -> t (h d)"),
@@ -135,47 +159,65 @@ def tile_multiqueryattention_pa_s_kernel(tc, x, sin, cos, w_qkv, q_rot, k_rot, v
                 )
 
         def rope_products(s):
-            first, width, heads, scale = steps[s]
-            u = acc[s][:, 0:heads, :]
-
-            def for_all_heads(table):
-                return table.unsqueeze(1).to_broadcast([P, heads, table.shape[1]])
-
-            nc.vector.scalar_tensor_tensor(
-                out=crossed[s][:, :, low], in0=u[:, :, high], scalar=-scale,
-                in1=for_all_heads(sin_sb[:, low]), op0=MULT, op1=MULT,
-            )
-            nc.vector.scalar_tensor_tensor(
-                out=crossed[s][:, :, high], in0=u[:, :, low], scalar=scale,
-                in1=for_all_heads(sin_sb[:, high]), op0=MULT, op1=MULT,
-            )
-            nc.vector.scalar_tensor_tensor(
-                out=straight[s][:], in0=u, scalar=scale,
-                in1=for_all_heads(cos_sb[:]), op0=MULT, op1=MULT,
+            first, width, heads = steps[s]
+            factors = k_factors if first == Q_COLS else q_factors
+            shape = [P, heads, 2, HEAD_DIM]
+            nc.vector.tensor_tensor(
+                out=products[s][:],
+                in0=acc[s][:, 0:heads, :].unsqueeze(2).to_broadcast(shape),
+                in1=factors[:].unsqueeze(1).to_broadcast(shape),
+                op=MULT,
             )
             if first == Q_COLS:
-                nc.vector.tensor_copy(out=v_sb[:], in_=acc[s][:, 1, :])
+                nc.scalar.copy(out=v_sb[:], in_=acc[s][:, 1, :])
+                nc.scalar.dma_start(out=v_out[0], in_=v_sb[:])
 
         def rope_sum_and_store(s):
-            first, width, heads, scale = steps[s]
-            nc.vector.tensor_tensor(out=rotated[s][:], in0=straight[s][:], in1=crossed[s][:], op=ADD)
+            first, width, heads = steps[s]
+            halves = products[s][:].rearrange("p h r (a d) -> p h r a d", a=2)
+            nc.vector.tensor_tensor(
+                out=rotated[s][:].rearrange("p h (a d) -> p h a d", a=2),
+                in0=halves[:, :, 0, :, :],
+                in1=halves[:, :, 1, ::-1, :],
+                op=ADD,
+            )
             if first == Q_COLS:
                 nc.sync.dma_start(out=k_rot[0], in_=rotated[s][:, 0, :])
-                nc.sync.dma_start(out=v_out[0], in_=v_sb[:])
             else:
                 head = first // HEAD_DIM
                 nc.sync.dma_start(
                     out=q_rot[0, head : head + heads].rearrange("h t d -> t h d"), in_=rotated[s][:]
                 )
 
-        for s in range(n_steps + 2):
-            if 1 <= s <= n_steps:
-                quantise_and_multiply(s - 1)
-            if s >= 2:
-                rope_products(s - 2)
-            if s < n_steps:
-                regroup_step(s)
-            if s == 0:
-                quantise_x()
-            if s >= 2:
-                rope_sum_and_store(s - 2)
+        for s in range(n_steps):
+            for g in range(PASSES):
+                regroup_scalar(s, g)
+
+        regroup_vector(0, 0)
+        regroup_vector(0, 1)
+        quantise_and_multiply(0)
+        regroup_vector(1, 0)
+        regroup_x()
+        regroup_vector(1, 1)
+        quantise_x()
+        multiply(0)
+        quantise_and_multiply(1)
+        multiply(1)
+        regroup_vector(2, 1)
+        rope_products(0)
+        quantise_and_multiply(2)
+        multiply(2)
+        rope_sum_and_store(0)
+        rope_products(1)
+        regroup_vector(3, 1)
+        rope_sum_and_store(1)
+        quantise_and_multiply(3)
+        multiply(3)
+        rope_products(2)
+        quantise_and_multiply(4)
+        multiply(4)
+        rope_sum_and_store(2)
+        rope_products(3)
+        rope_products(4)
+        rope_sum_and_store(3)
+        rope_sum_and_store(4)

@@ -24,7 +24,7 @@ N_COLS = Q_COLS + 2 * HEAD_DIM
 Q_SCALE = HEAD_DIM**-0.5
 
 STEP_COLS = 256
-RUN = 4
+RUN = 8
 VECTOR_PARTS = ((8, 8), (8, 8), (0, 8), (0, 4), (0, 0))
 
 FLOPS = 2 * P * K * N_COLS

@@ -24,7 +24,7 @@ N_COLS = Q_COLS + 2 * HEAD_DIM
 Q_SCALE = HEAD_DIM**-0.5
 
 STEP_COLS = 256
-RUN = 8
+RUN = 2
 VECTOR_PARTS = ((8, 8), (8, 8), (0, 8), (0, 4), (0, 0))
 
 FLOPS = 2 * P * K * N_COLS

from contextlib import ExitStack

import concourse.mybir as mybir
from concourse.masks import make_identity

BF16 = mybir.dt.bfloat16
F32 = mybir.dt.float32
U32 = mybir.dt.uint32
U8 = mybir.dt.uint8
FP8X4 = mybir.dt.float8_e4m3fn_x4
MULT = mybir.AluOpType.mult
ADD = mybir.AluOpType.add

P = 128
PACK = 4
K_PASS = P * PACK
K = 1024
PASSES = K // K_PASS
HEADS = 16
HEAD_DIM = 64
HALF = HEAD_DIM // 2
Q_COLS = HEADS * HEAD_DIM
N_COLS = Q_COLS + 2 * HEAD_DIM
Q_SCALE = HEAD_DIM**-0.5

STEP_COLS = 256
RUN = 2
VECTOR_PARTS = ((8, 8), (8, 8), (0, 8), (0, 4), (0, 0))

FLOPS = 2 * P * K * N_COLS


def interleaved(grouped):
    return grouped.rearrange("p (c i) j -> p c j i", i=RUN)


def rows(raw):
    return raw.rearrange("p j (c i) -> p c j i", i=RUN)


def tile_multiqueryattention_pa_s_kernel(tc, x, sin, cos, w_qkv, q_rot, k_rot, v_out):
    nc = tc.nc
    steps = []
    for first in range(0, Q_COLS, STEP_COLS):
        steps.append((first, STEP_COLS, STEP_COLS // HEAD_DIM))
    steps.append((Q_COLS, 2 * HEAD_DIM, 1))
    n_steps = len(steps)
    low = slice(0, HALF)
    high = slice(HALF, HEAD_DIM)

    with ExitStack() as ctx:
        keep = ctx.enter_context(tc.tile_pool(name="keep", bufs=1))
        psum = ctx.enter_context(tc.psum_pool(name="psum", bufs=1))
        ctx.enter_context(tc.manual_schedule())

        raw = []

        def load_step(s):
            first, width, heads = steps[s]
            tiles = []
            for g in range(PASSES):
                raw_pass = keep.tile([P, PACK, width], BF16, name="raw%d_%d" % (first, g))
                nc.sync.dma_start(
                    out=raw_pass[:],
                    in_=w_qkv[g * K_PASS : (g + 1) * K_PASS, first : first + width].rearrange(
                        "(p j) w -> p j w", j=PACK
                    ),
                )
                tiles.append(raw_pass)
            raw.append(tiles)

        load_step(0)
        x_sb = keep.tile([P, K], BF16)
        nc.sync.dma_start(out=x_sb[:], in_=x[0])
        cos_sb = keep.tile([P, HEAD_DIM], BF16)
        nc.scalar.dma_start(out=cos_sb[:], in_=cos)
        sin_sb = keep.tile([P, HEAD_DIM], BF16)
        nc.scalar.dma_start(out=sin_sb[:], in_=sin)
        for s in range(1, n_steps):
            load_step(s)

        identity = keep.tile([P, P], F32)
        make_identity(nc, identity[:])
        x_words = x_sb[:].bitcast(F32).rearrange("t (g p u) -> t g u p", g=PASSES, u=PACK // 2)
        x_turned = psum.tile([P, PASSES, PACK // 2, P], F32)
        for g in range(PASSES):
            for u in range(PACK // 2):
                nc.tensor.transpose(x_turned[:, g, u, :], x_words[:, g, u, :], identity[:])
        x_grouped = keep.tile([P, PASSES, P, PACK // 2], F32, align_bytes=64)
        x_codes = keep.tile([P, PASSES, P], U32, align_bytes=64)
        x_scales = keep.tile([P, PASSES, P], U8, align_bytes=64)

        def regroup_x():
            nc.vector.tensor_copy(out=x_grouped[:], in_=x_turned[:].rearrange("p g u t -> p g t u"))

        def quantise_x():
            nc.vector.quantize_mx(
                out=x_codes[:].rearrange("p g t -> p (g t)").bitcast(FP8X4),
                scales=x_scales[:].rearrange("p g t -> p (g t)"),
                in_=x_grouped[:].rearrange("p g t u -> p (g t u)").bitcast(BF16),
            )

        k_factors = keep.tile([P, 2, HEAD_DIM], F32)
        nc.gpsimd.tensor_copy(out=k_factors[:, 0, :], in_=cos_sb[:])
        nc.gpsimd.tensor_copy(out=k_factors[:, 1, low], in_=sin_sb[:, high])
        nc.gpsimd.tensor_scalar(
            out=k_factors[:, 1, high], in0=sin_sb[:, low], scalar1=-1.0, scalar2=0.0, op0=MULT, op1=ADD
        )
        q_factors = keep.tile([P, 2, HEAD_DIM], F32)
        nc.gpsimd.tensor_scalar(
            out=q_factors[:], in0=k_factors[:], scalar1=Q_SCALE, scalar2=0.0, op0=MULT, op1=ADD
        )

        grouped = []
        w_codes = []
        w_scales = []
        acc = []
        products = []
        rotated = []
        for first, width, heads in steps:
            grouped.append(keep.tile([P, PASSES, width, PACK], BF16, align_bytes=64, name="grouped%d" % first))
            w_codes.append(keep.tile([P, PASSES, width], U32, align_bytes=64, name="w_codes%d" % first))
            w_scales.append(keep.tile([P, PASSES, width], U8, align_bytes=64, name="w_scales%d" % first))
            acc.append(psum.tile([P, width // HEAD_DIM, HEAD_DIM], F32, name="acc%d" % first))
            products.append(keep.tile([P, heads, 2, HEAD_DIM], F32, name="products%d" % first))
            rotated.append(keep.tile([P, heads, HEAD_DIM], F32, name="rotated%d" % first))
        v_sb = keep.tile([P, HEAD_DIM], F32)

        def border(s, g):
            width = steps[s][1]
            return width - width * VECTOR_PARTS[s][g] // 16

        def regroup_scalar(s, g):
            b = border(s, g)
            nc.scalar.copy(out=interleaved(grouped[s][:, g, :b, :]), in_=rows(raw[s][g][:, :, :b]))

        def regroup_vector(s, g):
            b = border(s, g)
            if b < steps[s][1]:
                nc.vector.tensor_copy(out=interleaved(grouped[s][:, g, b:, :]), in_=rows(raw[s][g][:, :, b:]))

        def quantise_and_multiply(s):
            nc.vector.quantize_mx(
                out=w_codes[s][:].rearrange("p g w -> p (g w)").bitcast(FP8X4),
                scales=w_scales[s][:].rearrange("p g w -> p (g w)"),
                in_=grouped[s][:].rearrange("p g w j -> p (g w j)"),
            )

        def multiply(s):
            for g in range(PASSES):
                nc.tensor.matmul_mx(
                    out=acc[s][:].rearrange("t h d -> t (h d)"),
                    lhsT=x_codes[:, g, :].bitcast(FP8X4),
                    lhsT_scale=x_scales[:, g, :],
                    rhs=w_codes[s][:, g, :].bitcast(FP8X4),
                    rhs_scale=w_scales[s][:, g, :],
                    start=(g == 0),
                    stop=(g == PASSES - 1),
                )

        def rope_products(s):
            first, width, heads = steps[s]
            factors = k_factors if first == Q_COLS else q_factors
            shape = [P, heads, 2, HEAD_DIM]
            nc.vector.tensor_tensor(
                out=products[s][:],
                in0=acc[s][:, 0:heads, :].unsqueeze(2).to_broadcast(shape),
                in1=factors[:].unsqueeze(1).to_broadcast(shape),
                op=MULT,
            )
            if first == Q_COLS:
                nc.scalar.copy(out=v_sb[:], in_=acc[s][:, 1, :])
                nc.scalar.dma_start(out=v_out[0], in_=v_sb[:])

        def rope_sum_and_store(s):
            first, width, heads = steps[s]
            halves = products[s][:].rearrange("p h r (a d) -> p h r a d", a=2)
            nc.vector.tensor_tensor(
                out=rotated[s][:].rearrange("p h (a d) -> p h a d", a=2),
                in0=halves[:, :, 0, :, :],
                in1=halves[:, :, 1, ::-1, :],
                op=ADD,
            )
            if first == Q_COLS:
                nc.sync.dma_start(out=k_rot[0], in_=rotated[s][:, 0, :])
            else:
                head = first // HEAD_DIM
                nc.sync.dma_start(
                    out=q_rot[0, head : head + heads].rearrange("h t d -> t h d"), in_=rotated[s][:]
                )

        for s in range(n_steps):
            for g in range(PASSES):
                regroup_scalar(s, g)

        regroup_vector(0, 0)
        regroup_vector(0, 1)
        quantise_and_multiply(0)
        regroup_vector(1, 0)
        regroup_x()
        regroup_vector(1, 1)
        quantise_x()
        multiply(0)
        quantise_and_multiply(1)
        multiply(1)
        regroup_vector(2, 1)
        rope_products(0)
        quantise_and_multiply(2)
        multiply(2)
        rope_sum_and_store(0)
        rope_products(1)
        regroup_vector(3, 1)
        rope_sum_and_store(1)
        quantise_and_multiply(3)
        multiply(3)
        rope_products(2)
        quantise_and_multiply(4)
        multiply(4)
        rope_sum_and_store(2)
        rope_products(3)
        rope_products(4)
        rope_sum_and_store(3)
        rope_sum_and_store(4)
